import numpy as np
import ml_dtypes

BF16 = ml_dtypes.bfloat16


def bf(x):
    return np.asarray(x, np.float32).astype(BF16)


def f32(x):
    return np.asarray(x, np.float32)


def f64(x):
    return np.asarray(x).astype(np.float64)


def striped(idx):
    return np.tile(idx.reshape(-1, 16).T, (8, 1))


C, S, N = 256, 256, 128


def setup_inputs():
    return {
        "item_emb": f32(np.random.standard_normal((C, S))),
        "pos_emb": f32(0.5 * np.random.standard_normal((C, N))),
        "wk": bf(np.random.standard_normal((C, C)) / np.sqrt(C)),
        "bk": f32(0.1 * np.random.standard_normal((C, 1))),
        "wv": bf(np.random.standard_normal((C, C)) / np.sqrt(C)),
        "bv": f32(0.1 * np.random.standard_normal((C, 1))),
        "offs": striped(np.random.permutation(np.tile(np.arange(S), 2))[:N]),
    }


def reference(item_emb, pos_emb, wk, bk, wv, bv, offs):
    idx = offs[:16].T.reshape(-1)
    seq = f64(item_emb)[:, idx] + f64(pos_emb)
    keys = f64(wk).T @ seq + f64(bk)
    vals = f64(wv).T @ seq + f64(bv)
    return np.concatenate([seq, keys, vals], axis=0)

@@ -1,0 +1,64 @@
+import concourse.mybir as mybir
+
+P = 128
+C, S, N = 256, 256, 128
+CB = C // P
+F32, BF16, U16 = mybir.dt.float32, mybir.dt.bfloat16, mybir.dt.uint16
+
+FLOPS = 2 * (2 * C) * C * N
+
+
+def tile_att_diffuse_model_kernel(tc, item_emb, pos_emb, wk, bk, wv, bv, offs, out):
+    nc = tc.nc
+    add = mybir.AluOpType.add
+    identity = mybir.ActivationFunctionType.Identity
+
+    with (
+        tc.tile_pool(name="held", bufs=1) as held,
+        tc.psum_pool(name="psum", bufs=1) as psum,
+    ):
+        offsets = held.tile([P, N // 16], U16, name="offsets")
+        nc.sync.dma_start(offsets[:], offs)
+
+        items = [held.tile([P, S], F32, name=f"items{cb}") for cb in range(CB)]
+        pos = [held.tile([P, N], F32, name=f"pos{cb}") for cb in range(CB)]
+        for cb in range(CB):
+            rows = slice(cb * P, (cb + 1) * P)
+            nc.sync.dma_start(items[cb][:], item_emb[rows, :])
+            nc.scalar.dma_start(pos[cb][:], pos_emb[rows, :])
+
+        weights = {}
+        for name, w in (("k", wk), ("v", wv)):
+            weights[name] = held.tile([P, CB, C], BF16, name=f"w{name}")
+            nc.scalar.dma_start(weights[name][:], w.rearrange("(kb p) m -> p kb m", p=P))
+
+        biases = {}
+        for name, b in (("k", bk), ("v", bv)):
+            biases[name] = held.tile([P, CB], F32, name=f"b{name}")
+            with nc.allow_non_contiguous_dma(reason="256 biases, one to a partition and block"):
+                nc.sync.dma_start(biases[name][:], b.rearrange("(mb p) o -> p (mb o)", p=P))
+
+        seq_bf = []
+        for cb in range(CB):
+            seq = held.tile([P, N], F32, name=f"seq{cb}")
+            nc.vector.tensor_tensor(seq[:], items[cb][:].indirect(offsets[:]), pos[cb][:], add)
+            nc.sync.dma_start(out[cb * P : (cb + 1) * P, :], seq[:])
+            rounded = held.tile([P, N], BF16, name=f"seq_bf{cb}")
+            nc.vector.tensor_copy(rounded[:], seq[:])
+            seq_bf.append(rounded)
+
+        for part, name in enumerate(("k", "v")):
+            for mb in range(CB):
+                product = psum.tile([P, N], F32, name=f"product_{name}{mb}")
+                for kb in range(CB):
+                    nc.tensor.matmul(
+                        product[:],
+                        weights[name][:, kb, mb * P : (mb + 1) * P],
+                        seq_bf[kb][:],
+                        start=(kb == 0),
+                        stop=(kb == CB - 1),
+                    )
+                biased = held.tile([P, N], F32, name=f"biased_{name}{mb}")
+                nc.scalar.activation(biased[:], product[:], identity, bias=biases[name][:, mb : mb + 1])
+                first_row = (1 + part) * C + mb * P
+                nc.sync.dma_start(out[first_row : first_row + P, :], biased[:])

@@ -17,48 +17,44 @@ def tile_att_diffuse_model_kernel(tc, item_emb, pos_emb, wk, bk, wv, bv, offs, o
         tc.tile_pool(name="held", bufs=1) as held,
         tc.psum_pool(name="psum", bufs=1) as psum,
     ):
-        offsets = held.tile([P, N // 16], U16, name="offsets")
-        nc.sync.dma_start(offsets[:], offs)
-
         items = [held.tile([P, S], F32, name=f"items{cb}") for cb in range(CB)]
-        pos = [held.tile([P, N], F32, name=f"pos{cb}") for cb in range(CB)]
-        for cb in range(CB):
-            rows = slice(cb * P, (cb + 1) * P)
-            nc.sync.dma_start(items[cb][:], item_emb[rows, :])
-            nc.scalar.dma_start(pos[cb][:], pos_emb[rows, :])
+        offsets = held.tile([P, N // 16], U16, name="offsets")
+        pos = held.tile([P, CB, N], F32, name="pos")
+        nc.sync.dma_start(items[0][:], item_emb[0:P, :])
+        nc.sync.dma_start(offsets[:], offs)
+        nc.scalar.dma_start(pos[:], pos_emb.rearrange("(cb p) n -> p cb n", p=P))
+        nc.scalar.dma_start(items[1][:], item_emb[P : 2 * P, :])
 
         weights = {}
         for name, w in (("k", wk), ("v", wv)):
             weights[name] = held.tile([P, CB, C], BF16, name=f"w{name}")
-            nc.scalar.dma_start(weights[name][:], w.rearrange("(kb p) m -> p kb m", p=P))
+            nc.gpsimd.dma_start(weights[name][:], w.rearrange("(kb p) m -> p kb m", p=P))
 
         biases = {}
         for name, b in (("k", bk), ("v", bv)):
             biases[name] = held.tile([P, CB], F32, name=f"b{name}")
             with nc.allow_non_contiguous_dma(reason="256 biases, one to a partition and block"):
-                nc.sync.dma_start(biases[name][:], b.rearrange("(mb p) o -> p (mb o)", p=P))
+                nc.gpsimd.dma_start(biases[name][:], b.rearrange("(mb p) o -> p (mb o)", p=P))
 
-        seq_bf = []
-        for cb in range(CB):
-            seq = held.tile([P, N], F32, name=f"seq{cb}")
-            nc.vector.tensor_tensor(seq[:], items[cb][:].indirect(offsets[:]), pos[cb][:], add)
-            nc.sync.dma_start(out[cb * P : (cb + 1) * P, :], seq[:])
-            rounded = held.tile([P, N], BF16, name=f"seq_bf{cb}")
-            nc.vector.tensor_copy(rounded[:], seq[:])
-            seq_bf.append(rounded)
+        blocks = [(name, mb) for name in ("k", "v") for mb in range(CB)]
+        products = [psum.tile([P, N], F32, name=f"product_{name}{mb}") for name, mb in blocks]
 
-        for part, name in enumerate(("k", "v")):
-            for mb in range(CB):
-                product = psum.tile([P, N], F32, name=f"product_{name}{mb}")
-                for kb in range(CB):
-                    nc.tensor.matmul(
-                        product[:],
-                        weights[name][:, kb, mb * P : (mb + 1) * P],
-                        seq_bf[kb][:],
-                        start=(kb == 0),
-                        stop=(kb == CB - 1),
-                    )
-                biased = held.tile([P, N], F32, name=f"biased_{name}{mb}")
-                nc.scalar.activation(biased[:], product[:], identity, bias=biases[name][:, mb : mb + 1])
-                first_row = (1 + part) * C + mb * P
-                nc.sync.dma_start(out[first_row : first_row + P, :], biased[:])
+        for kb in range(CB):
+            seq = held.tile([P, N], F32, name=f"seq{kb}")
+            nc.vector.tensor_tensor(seq[:], items[kb][:].indirect(offsets[:]), pos[:, kb, :], add)
+            nc.sync.dma_start(out[kb * P : (kb + 1) * P, :], seq[:])
+            seq_bf = held.tile([P, N], BF16, name=f"seq_bf{kb}")
+            nc.vector.tensor_copy(seq_bf[:], seq[:])
+            for product, (name, mb) in zip(products, blocks):
+                nc.tensor.matmul(
+                    product[:],
+                    weights[name][:, kb, mb * P : (mb + 1) * P],
+                    seq_bf[:],
+                    start=(kb == 0),
+                    stop=(kb == CB - 1),
+                )
+
+        for b, (product, (name, mb)) in enumerate(zip(products, blocks)):
+            biased = held.tile([P, N], F32, name=f"biased_{name}{mb}")
+            nc.scalar.activation(biased[:], product[:], identity, bias=biases[name][:, mb : mb + 1])
+            nc.sync.dma_start(out[C + b * P : C + (b + 1) * P, :], biased[:])

@@ -11,7 +11,6 @@ FLOPS = 2 * (2 * C) * C * N
 def tile_att_diffuse_model_kernel(tc, item_emb, pos_emb, wk, bk, wv, bv, offs, out):
     nc = tc.nc
     add = mybir.AluOpType.add
-    identity = mybir.ActivationFunctionType.Identity
 
     with (
         tc.tile_pool(name="held", bufs=1) as held,
@@ -25,36 +24,42 @@ def tile_att_diffuse_model_kernel(tc, item_emb, pos_emb, wk, bk, wv, bv, offs, o
         nc.scalar.dma_start(pos[:], pos_emb.rearrange("(cb p) n -> p cb n", p=P))
         nc.scalar.dma_start(items[1][:], item_emb[P : 2 * P, :])
 
+        queues = {"k": nc.sync, "v": nc.scalar}
+
         weights = {}
         for name, w in (("k", wk), ("v", wv)):
             weights[name] = held.tile([P, CB, C], BF16, name=f"w{name}")
-            nc.gpsimd.dma_start(weights[name][:], w.rearrange("(kb p) m -> p kb m", p=P))
+            queues[name].dma_start(weights[name][:], w.rearrange("(kb p) m -> p kb m", p=P))
 
         biases = {}
         for name, b in (("k", bk), ("v", bv)):
             biases[name] = held.tile([P, CB], F32, name=f"b{name}")
             with nc.allow_non_contiguous_dma(reason="256 biases, one to a partition and block"):
-                nc.gpsimd.dma_start(biases[name][:], b.rearrange("(mb p) o -> p (mb o)", p=P))
+                queues[name].dma_start(biases[name][:], b.rearrange("(mb p) o -> p (mb o)", p=P))
 
         blocks = [(name, mb) for name in ("k", "v") for mb in range(CB)]
-        products = [psum.tile([P, N], F32, name=f"product_{name}{mb}") for name, mb in blocks]
+        products = {block: psum.tile([P, N], F32, name=f"product_{block[0]}{block[1]}") for block in blocks}
 
         for kb in range(CB):
             seq = held.tile([P, N], F32, name=f"seq{kb}")
             nc.vector.tensor_tensor(seq[:], items[kb][:].indirect(offsets[:]), pos[:, kb, :], add)
-            nc.sync.dma_start(out[kb * P : (kb + 1) * P, :], seq[:])
+            (nc.sync, nc.scalar)[kb].dma_start(out[kb * P : (kb + 1) * P, :], seq[:])
             seq_bf = held.tile([P, N], BF16, name=f"seq_bf{kb}")
             nc.vector.tensor_copy(seq_bf[:], seq[:])
-            for product, (name, mb) in zip(products, blocks):
+            for name, mb in blocks:
                 nc.tensor.matmul(
-                    product[:],
+                    products[name, mb][:],
                     weights[name][:, kb, mb * P : (mb + 1) * P],
                     seq_bf[:],
                     start=(kb == 0),
                     stop=(kb == CB - 1),
                 )
 
-        for b, (product, (name, mb)) in enumerate(zip(products, blocks)):
-            biased = held.tile([P, N], F32, name=f"biased_{name}{mb}")
-            nc.scalar.activation(biased[:], product[:], identity, bias=biases[name][:, mb : mb + 1])
-            nc.sync.dma_start(out[C + b * P : C + (b + 1) * P, :], biased[:])
+        for part, name in enumerate(("k", "v")):
+            biased = held.tile([P, CB, N], F32, name=f"biased_{name}")
+            for mb in range(CB):
+                nc.vector.tensor_scalar(
+                    biased[:, mb, :], products[name, mb][:], biases[name][:, mb : mb + 1], None, add
+                )
+            rows = out[(1 + part) * C : (2 + part) * C, :]
+            queues[name].dma_start(rows.rearrange("(mb p) n -> p mb n", p=P), biased[:])

@@ -5,6 +5,9 @@ C, S, N = 256, 256, 128
 CB = C // P
 F32, BF16, U16 = mybir.dt.float32, mybir.dt.bfloat16, mybir.dt.uint16
 
+WARM_COLUMNS = 512
+WARM_MATMULS = 5
+
 FLOPS = 2 * (2 * C) * C * N
 
 
@@ -16,50 +19,53 @@ def tile_att_diffuse_model_kernel(tc, item_emb, pos_emb, wk, bk, wv, bv, offs, o
         tc.tile_pool(name="held", bufs=1) as held,
         tc.psum_pool(name="psum", bufs=1) as psum,
     ):
+
         items = [held.tile([P, S], F32, name=f"items{cb}") for cb in range(CB)]
         offsets = held.tile([P, N // 16], U16, name="offsets")
         pos = held.tile([P, CB, N], F32, name="pos")
-        nc.sync.dma_start(items[0][:], item_emb[0:P, :])
+        item_blocks = item_emb.rearrange("(p cb) s -> p cb s", cb=CB)
+        nc.sync.dma_start(items[0][:], item_blocks[:, 0, :])
         nc.sync.dma_start(offsets[:], offs)
-        nc.scalar.dma_start(pos[:], pos_emb.rearrange("(cb p) n -> p cb n", p=P))
-        nc.scalar.dma_start(items[1][:], item_emb[P : 2 * P, :])
+        nc.scalar.dma_start(pos[:], pos_emb.rearrange("(p cb) n -> p cb n", cb=CB))
+        nc.scalar.dma_start(items[1][:], item_blocks[:, 1, :])
 
-        queues = {"k": nc.sync, "v": nc.scalar}
-
+        load_queues = {"k": nc.sync, "v": nc.scalar}
         weights = {}
         for name, w in (("k", wk), ("v", wv)):
             weights[name] = held.tile([P, CB, C], BF16, name=f"w{name}")
-            queues[name].dma_start(weights[name][:], w.rearrange("(kb p) m -> p kb m", p=P))
+            load_queues[name].dma_start(weights[name][:], w.rearrange("(p cb) m -> p cb m", cb=CB))
 
         biases = {}
         for name, b in (("k", bk), ("v", bv)):
             biases[name] = held.tile([P, CB], F32, name=f"b{name}")
             with nc.allow_non_contiguous_dma(reason="256 biases, one to a partition and block"):
-                queues[name].dma_start(biases[name][:], b.rearrange("(mb p) o -> p (mb o)", p=P))
+                load_queues[name].dma_start(biases[name][:], b.rearrange("(mb p) o -> p (mb o)", p=P))
 
-        blocks = [(name, mb) for name in ("k", "v") for mb in range(CB)]
-        products = {block: psum.tile([P, N], F32, name=f"product_{block[0]}{block[1]}") for block in blocks}
+        zeros = held.tile([P, WARM_COLUMNS], BF16, name="zeros")
+        nc.vector.memset(zeros[:], 0.0)
+        unused = psum.tile([P, WARM_COLUMNS], F32, name="unused")
+        for repeat in range(WARM_MATMULS):
+            nc.tensor.matmul(unused[:], zeros[:, 0:P], zeros[:], start=True, stop=True)
 
-        for kb in range(CB):
-            seq = held.tile([P, N], F32, name=f"seq{kb}")
-            nc.vector.tensor_tensor(seq[:], items[kb][:].indirect(offsets[:]), pos[:, kb, :], add)
-            (nc.sync, nc.scalar)[kb].dma_start(out[kb * P : (kb + 1) * P, :], seq[:])
-            seq_bf = held.tile([P, N], BF16, name=f"seq_bf{kb}")
-            nc.vector.tensor_copy(seq_bf[:], seq[:])
-            for name, mb in blocks:
-                nc.tensor.matmul(
-                    products[name, mb][:],
-                    weights[name][:, kb, mb * P : (mb + 1) * P],
-                    seq_bf[:],
-                    start=(kb == 0),
-                    stop=(kb == CB - 1),
-                )
+        seq = held.tile([P, CB, N], F32, name="seq")
+        for cb in range(CB):
+            nc.vector.tensor_tensor(seq[:, cb, :], items[cb][:].indirect(offsets[:]), pos[:, cb, :], add)
+        nc.sync.dma_start(out[0:C, :].rearrange("(p cb) n -> p cb n", cb=CB), seq[:])
+        seq_bf = held.tile([P, CB, N], BF16, name="seq_bf")
+        nc.vector.tensor_copy(seq_bf[:], seq[:])
 
-        for part, name in enumerate(("k", "v")):
+        for part, (name, store_queue) in enumerate((("k", nc.scalar), ("v", nc.sync))):
             biased = held.tile([P, CB, N], F32, name=f"biased_{name}")
             for mb in range(CB):
-                nc.vector.tensor_scalar(
-                    biased[:, mb, :], products[name, mb][:], biases[name][:, mb : mb + 1], None, add
-                )
+                product = psum.tile([P, N], F32, name=f"product_{name}{mb}")
+                for cb in range(CB):
+                    nc.tensor.matmul(
+                        product[:],
+                        weights[name][:, cb, mb * P : (mb + 1) * P],
+                        seq_bf[:, cb, :],
+                        start=(cb == 0),
+                        stop=(cb == CB - 1),
+                    )
+                nc.vector.tensor_scalar(biased[:, mb, :], product[:], biases[name][:, mb : mb + 1], None, add)
             rows = out[(1 + part) * C : (2 + part) * C, :]
-            queues[name].dma_start(rows.rearrange("(mb p) n -> p mb n", p=P), biased[:])
+            store_queue.dma_start(rows.rearrange("(mb p) n -> p mb n", p=P), biased[:])

@@ -5,9 +5,6 @@ C, S, N = 256, 256, 128
 CB = C // P
 F32, BF16, U16 = mybir.dt.float32, mybir.dt.bfloat16, mybir.dt.uint16
 
-WARM_COLUMNS = 512
-WARM_MATMULS = 5
-
 FLOPS = 2 * (2 * C) * C * N
 
 
@@ -40,12 +37,6 @@ def tile_att_diffuse_model_kernel(tc, item_emb, pos_emb, wk, bk, wv, bv, offs, o
             biases[name] = held.tile([P, CB], F32, name=f"b{name}")
             with nc.allow_non_contiguous_dma(reason="256 biases, one to a partition and block"):
                 load_queues[name].dma_start(biases[name][:], b.rearrange("(mb p) o -> p (mb o)", p=P))
-
-        zeros = held.tile([P, WARM_COLUMNS], BF16, name="zeros")
-        nc.vector.memset(zeros[:], 0.0)
-        unused = psum.tile([P, WARM_COLUMNS], F32, name="unused")
-        for repeat in range(WARM_MATMULS):
-            nc.tensor.matmul(unused[:], zeros[:, 0:P], zeros[:], start=True, stop=True)
 
         seq = held.tile([P, CB, N], F32, name="seq")
         for cb in range(CB):

@@ -5,6 +5,9 @@ C, S, N = 256, 256, 128
 CB = C // P
 F32, BF16, U16 = mybir.dt.float32, mybir.dt.bfloat16, mybir.dt.uint16
 
+WARM_COLUMNS = 512
+WARM_MATMULS = 5
+
 FLOPS = 2 * (2 * C) * C * N
 
 
@@ -16,47 +19,51 @@ def tile_att_diffuse_model_kernel(tc, item_emb, pos_emb, wk, bk, wv, bv, offs, o
         tc.tile_pool(name="held", bufs=1) as held,
         tc.psum_pool(name="psum", bufs=1) as psum,
     ):
-
         items = [held.tile([P, S], F32, name=f"items{cb}") for cb in range(CB)]
         offsets = held.tile([P, N // 16], U16, name="offsets")
         pos = held.tile([P, CB, N], F32, name="pos")
-        item_blocks = item_emb.rearrange("(p cb) s -> p cb s", cb=CB)
-        nc.sync.dma_start(items[0][:], item_blocks[:, 0, :])
+        nc.sync.dma_start(items[0][:], item_emb[0:P, :])
         nc.sync.dma_start(offsets[:], offs)
-        nc.scalar.dma_start(pos[:], pos_emb.rearrange("(p cb) n -> p cb n", cb=CB))
-        nc.scalar.dma_start(items[1][:], item_blocks[:, 1, :])
+        nc.scalar.dma_start(pos[:], pos_emb.rearrange("(cb p) n -> p cb n", p=P))
+        nc.scalar.dma_start(items[1][:], item_emb[P : 2 * P, :])
 
         load_queues = {"k": nc.sync, "v": nc.scalar}
         weights = {}
         for name, w in (("k", wk), ("v", wv)):
             weights[name] = held.tile([P, CB, C], BF16, name=f"w{name}")
-            load_queues[name].dma_start(weights[name][:], w.rearrange("(p cb) m -> p cb m", cb=CB))
-
+            load_queues[name].dma_start(weights[name][:], w.rearrange("(cb p) m -> p cb m", p=P))
         biases = {}
         for name, b in (("k", bk), ("v", bv)):
             biases[name] = held.tile([P, CB], F32, name=f"b{name}")
             with nc.allow_non_contiguous_dma(reason="256 biases, one to a partition and block"):
                 load_queues[name].dma_start(biases[name][:], b.rearrange("(mb p) o -> p (mb o)", p=P))
 
+        zeros = held.tile([P, WARM_COLUMNS], BF16, name="zeros")
+        nc.vector.memset(zeros[:], 0.0)
+        unused = psum.tile([P, WARM_COLUMNS], F32, name="unused")
+        for repeat in range(WARM_MATMULS):
+            nc.tensor.matmul(unused[:], zeros[:, 0:P], zeros[:], start=True, stop=True)
+
         seq = held.tile([P, CB, N], F32, name="seq")
+        seq_bf = [held.tile([P, N], BF16, name=f"seq_bf{cb}") for cb in range(CB)]
         for cb in range(CB):
             nc.vector.tensor_tensor(seq[:, cb, :], items[cb][:].indirect(offsets[:]), pos[:, cb, :], add)
-        nc.sync.dma_start(out[0:C, :].rearrange("(p cb) n -> p cb n", cb=CB), seq[:])
-        seq_bf = held.tile([P, CB, N], BF16, name="seq_bf")
-        nc.vector.tensor_copy(seq_bf[:], seq[:])
+            nc.vector.tensor_copy(seq_bf[cb][:], seq[:, cb, :])
+        nc.sync.dma_start(out[0:C, :].rearrange("(cb p) n -> p cb n", p=P), seq[:])
 
         for part, (name, store_queue) in enumerate((("k", nc.scalar), ("v", nc.sync))):
-            biased = held.tile([P, CB, N], F32, name=f"biased_{name}")
-            for mb in range(CB):
-                product = psum.tile([P, N], F32, name=f"product_{name}{mb}")
-                for cb in range(CB):
+            products = [psum.tile([P, N], F32, name=f"product_{name}{mb}") for mb in range(CB)]
+            for cb in range(CB):
+                for mb in range(CB):
                     nc.tensor.matmul(
-                        product[:],
+                        products[mb][:],
                         weights[name][:, cb, mb * P : (mb + 1) * P],
-                        seq_bf[:, cb, :],
+                        seq_bf[cb][:],
                         start=(cb == 0),
                         stop=(cb == CB - 1),
                     )
-                nc.vector.tensor_scalar(biased[:, mb, :], product[:], biases[name][:, mb : mb + 1], None, add)
+            biased = held.tile([P, CB, N], F32, name=f"biased_{name}")
+            for mb in range(CB):
+                nc.vector.tensor_scalar(biased[:, mb, :], products[mb][:], biases[name][:, mb : mb + 1], None, add)
             rows = out[(1 + part) * C : (2 + part) * C, :]
             store_queue.dma_start(rows.rearrange("(mb p) n -> p mb n", p=P), biased[:])

@@ -27,16 +27,18 @@ def tile_att_diffuse_model_kernel(tc, item_emb, pos_emb, wk, bk, wv, bv, offs, o
         nc.scalar.dma_start(pos[:], pos_emb.rearrange("(cb p) n -> p cb n", p=P))
         nc.scalar.dma_start(items[1][:], item_emb[P : 2 * P, :])
 
-        load_queues = {"k": nc.sync, "v": nc.scalar}
+        queues = {"k": nc.sync, "v": nc.scalar}
+
         weights = {}
         for name, w in (("k", wk), ("v", wv)):
             weights[name] = held.tile([P, CB, C], BF16, name=f"w{name}")
-            load_queues[name].dma_start(weights[name][:], w.rearrange("(cb p) m -> p cb m", p=P))
+            queues[name].dma_start(weights[name][:], w.rearrange("(kb p) m -> p kb m", p=P))
+
         biases = {}
         for name, b in (("k", bk), ("v", bv)):
             biases[name] = held.tile([P, CB], F32, name=f"b{name}")
             with nc.allow_non_contiguous_dma(reason="256 biases, one to a partition and block"):
-                load_queues[name].dma_start(biases[name][:], b.rearrange("(mb p) o -> p (mb o)", p=P))
+                queues[name].dma_start(biases[name][:], b.rearrange("(mb p) o -> p (mb o)", p=P))
 
         zeros = held.tile([P, WARM_COLUMNS], BF16, name="zeros")
         nc.vector.memset(zeros[:], 0.0)
@@ -44,26 +46,29 @@ def tile_att_diffuse_model_kernel(tc, item_emb, pos_emb, wk, bk, wv, bv, offs, o
         for repeat in range(WARM_MATMULS):
             nc.tensor.matmul(unused[:], zeros[:, 0:P], zeros[:], start=True, stop=True)
 
-        seq = held.tile([P, CB, N], F32, name="seq")
-        seq_bf = [held.tile([P, N], BF16, name=f"seq_bf{cb}") for cb in range(CB)]
-        for cb in range(CB):
-            nc.vector.tensor_tensor(seq[:, cb, :], items[cb][:].indirect(offsets[:]), pos[:, cb, :], add)
-            nc.vector.tensor_copy(seq_bf[cb][:], seq[:, cb, :])
-        nc.sync.dma_start(out[0:C, :].rearrange("(cb p) n -> p cb n", p=P), seq[:])
+        blocks = [(name, mb) for name in ("k", "v") for mb in range(CB)]
+        products = {block: psum.tile([P, N], F32, name=f"product_{block[0]}{block[1]}") for block in blocks}
 
-        for part, (name, store_queue) in enumerate((("k", nc.scalar), ("v", nc.sync))):
-            products = [psum.tile([P, N], F32, name=f"product_{name}{mb}") for mb in range(CB)]
-            for cb in range(CB):
-                for mb in range(CB):
-                    nc.tensor.matmul(
-                        products[mb][:],
-                        weights[name][:, cb, mb * P : (mb + 1) * P],
-                        seq_bf[cb][:],
-                        start=(cb == 0),
-                        stop=(cb == CB - 1),
-                    )
+        for kb in range(CB):
+            seq = held.tile([P, N], F32, name=f"seq{kb}")
+            nc.vector.tensor_tensor(seq[:], items[kb][:].indirect(offsets[:]), pos[:, kb, :], add)
+            (nc.sync, nc.scalar)[kb].dma_start(out[kb * P : (kb + 1) * P, :], seq[:])
+            seq_bf = held.tile([P, N], BF16, name=f"seq_bf{kb}")
+            nc.vector.tensor_copy(seq_bf[:], seq[:])
+            for name, mb in blocks:
+                nc.tensor.matmul(
+                    products[name, mb][:],
+                    weights[name][:, kb, mb * P : (mb + 1) * P],
+                    seq_bf[:],
+                    start=(kb == 0),
+                    stop=(kb == CB - 1),
+                )
+
+        for part, name in enumerate(("k", "v")):
             biased = held.tile([P, CB, N], F32, name=f"biased_{name}")
             for mb in range(CB):
-                nc.vector.tensor_scalar(biased[:, mb, :], products[mb][:], biases[name][:, mb : mb + 1], None, add)
+                nc.vector.tensor_scalar(
+                    biased[:, mb, :], products[name, mb][:], biases[name][:, mb : mb + 1], None, add
+                )
             rows = out[(1 + part) * C : (2 + part) * C, :]
-            store_queue.dma_start(rows.rearrange("(mb p) n -> p mb n", p=P), biased[:])
+            queues[name].dma_start(rows.rearrange("(mb p) n -> p mb n", p=P), biased[:])

@@ -14,6 +14,7 @@ FLOPS = 2 * (2 * C) * C * N
 def tile_att_diffuse_model_kernel(tc, item_emb, pos_emb, wk, bk, wv, bv, offs, out):
     nc = tc.nc
     add = mybir.AluOpType.add
+    identity = mybir.ActivationFunctionType.Identity
 
     with (
         tc.tile_pool(name="held", bufs=1) as held,
@@ -46,6 +47,9 @@ def tile_att_diffuse_model_kernel(tc, item_emb, pos_emb, wk, bk, wv, bv, offs, o
         for repeat in range(WARM_MATMULS):
             nc.tensor.matmul(unused[:], zeros[:, 0:P], zeros[:], start=True, stop=True)
 
+        unused_column = held.tile([P, 1], F32, name="unused_column")
+        nc.scalar.activation(unused_column[:], zeros[:, 0:1], identity)
+
         blocks = [(name, mb) for name in ("k", "v") for mb in range(CB)]
         products = {block: psum.tile([P, N], F32, name=f"product_{block[0]}{block[1]}") for block in blocks}
 
@@ -67,8 +71,10 @@ def tile_att_diffuse_model_kernel(tc, item_emb, pos_emb, wk, bk, wv, bv, offs, o
         for part, name in enumerate(("k", "v")):
             biased = held.tile([P, CB, N], F32, name=f"biased_{name}")
             for mb in range(CB):
-                nc.vector.tensor_scalar(
-                    biased[:, mb, :], products[name, mb][:], biases[name][:, mb : mb + 1], None, add
-                )
+                bias = biases[name][:, mb : mb + 1]
+                if name == "k":
+                    nc.vector.tensor_scalar(biased[:, mb, :], products[name, mb][:], bias, None, add)
+                else:
+                    nc.scalar.activation(biased[:, mb, :], products[name, mb][:], identity, bias=bias)
             rows = out[(1 + part) * C : (2 + part) * C, :]
             queues[name].dma_start(rows.rearrange("(mb p) n -> p mb n", p=P), biased[:])

@@ -53,12 +53,14 @@ def tile_att_diffuse_model_kernel(tc, item_emb, pos_emb, wk, bk, wv, bv, offs, o
         blocks = [(name, mb) for name in ("k", "v") for mb in range(CB)]
         products = {block: psum.tile([P, N], F32, name=f"product_{block[0]}{block[1]}") for block in blocks}
 
+        seq = [held.tile([P, N], F32, name=f"seq{cb}") for cb in range(CB)]
+        for cb in range(CB):
+            nc.vector.tensor_tensor(seq[cb][:], items[cb][:].indirect(offsets[:]), pos[:, cb, :], add)
+            (nc.sync, nc.scalar)[cb].dma_start(out[cb * P : (cb + 1) * P, :], seq[cb][:])
+
         for kb in range(CB):
-            seq = held.tile([P, N], F32, name=f"seq{kb}")
-            nc.vector.tensor_tensor(seq[:], items[kb][:].indirect(offsets[:]), pos[:, kb, :], add)
-            (nc.sync, nc.scalar)[kb].dma_start(out[kb * P : (kb + 1) * P, :], seq[:])
             seq_bf = held.tile([P, N], BF16, name=f"seq_bf{kb}")
-            nc.vector.tensor_copy(seq_bf[:], seq[:])
+            nc.vector.tensor_copy(seq_bf[:], seq[kb][:])
             for name, mb in blocks:
                 nc.tensor.matmul(
                     products[name, mb][:],

@@ -38,8 +38,7 @@ def tile_att_diffuse_model_kernel(tc, item_emb, pos_emb, wk, bk, wv, bv, offs, o
         biases = {}
         for name, b in (("k", bk), ("v", bv)):
             biases[name] = held.tile([P, CB], F32, name=f"b{name}")
-            with nc.allow_non_contiguous_dma(reason="256 biases, one to a partition and block"):
-                queues[name].dma_start(biases[name][:], b.rearrange("(mb p) o -> p (mb o)", p=P))
+            queues[name].dma_start(biases[name][:], b.rearrange("(p mb) o -> p (mb o)", p=P))
 
         zeros = held.tile([P, WARM_COLUMNS], BF16, name="zeros")
         nc.vector.memset(zeros[:], 0.0)
@@ -64,7 +63,7 @@ def tile_att_diffuse_model_kernel(tc, item_emb, pos_emb, wk, bk, wv, bv, offs, o
             for name, mb in blocks:
                 nc.tensor.matmul(
                     products[name, mb][:],
-                    weights[name][:, kb, mb * P : (mb + 1) * P],
+                    weights[name][:, kb, mb::CB],
                     seq_bf[:],
                     start=(kb == 0),
                     stop=(kb == CB - 1),
@@ -79,4 +78,4 @@ def tile_att_diffuse_model_kernel(tc, item_emb, pos_emb, wk, bk, wv, bv, offs, o
                 else:
                     nc.scalar.activation(biased[:, mb, :], products[name, mb][:], identity, bias=bias)
             rows = out[(1 + part) * C : (2 + part) * C, :]
-            queues[name].dma_start(rows.rearrange("(mb p) n -> p mb n", p=P), biased[:])
+            queues[name].dma_start(rows.rearrange("(p mb) n -> p mb n", p=P), biased[:])

@@ -20,20 +20,21 @@ def tile_att_diffuse_model_kernel(tc, item_emb, pos_emb, wk, bk, wv, bv, offs, o
         tc.tile_pool(name="held", bufs=1) as held,
         tc.psum_pool(name="psum", bufs=1) as psum,
     ):
+        item_rows = item_emb.rearrange("(p cb) s -> p cb s", p=P)
         items = [held.tile([P, S], F32, name=f"items{cb}") for cb in range(CB)]
         offsets = held.tile([P, N // 16], U16, name="offsets")
         pos = held.tile([P, CB, N], F32, name="pos")
-        nc.sync.dma_start(items[0][:], item_emb[0:P, :])
+        nc.sync.dma_start(items[0][:], item_rows[:, 0, :])
         nc.sync.dma_start(offsets[:], offs)
-        nc.scalar.dma_start(pos[:], pos_emb.rearrange("(cb p) n -> p cb n", p=P))
-        nc.scalar.dma_start(items[1][:], item_emb[P : 2 * P, :])
+        nc.scalar.dma_start(pos[:], pos_emb.rearrange("(p cb) n -> p cb n", p=P))
+        nc.scalar.dma_start(items[1][:], item_rows[:, 1, :])
 
         queues = {"k": nc.sync, "v": nc.scalar}
 
         weights = {}
         for name, w in (("k", wk), ("v", wv)):
             weights[name] = held.tile([P, CB, C], BF16, name=f"w{name}")
-            queues[name].dma_start(weights[name][:], w.rearrange("(kb p) m -> p kb m", p=P))
+            queues[name].dma_start(weights[name][:], w.rearrange("(p kb) m -> p kb m", p=P))
 
         biases = {}
         for name, b in (("k", bk), ("v", bv)):
@@ -52,10 +53,11 @@ def tile_att_diffuse_model_kernel(tc, item_emb, pos_emb, wk, bk, wv, bv, offs, o
         blocks = [(name, mb) for name in ("k", "v") for mb in range(CB)]
         products = {block: psum.tile([P, N], F32, name=f"product_{block[0]}{block[1]}") for block in blocks}
 
+        seq_rows = out[0:C, :].rearrange("(p cb) n -> p cb n", p=P)
         seq = [held.tile([P, N], F32, name=f"seq{cb}") for cb in range(CB)]
         for cb in range(CB):
             nc.vector.tensor_tensor(seq[cb][:], items[cb][:].indirect(offsets[:]), pos[:, cb, :], add)
-            (nc.sync, nc.scalar)[cb].dma_start(out[cb * P : (cb + 1) * P, :], seq[cb][:])
+            (nc.sync, nc.scalar)[cb].dma_start(seq_rows[:, cb, :], seq[cb][:])
 
         for kb in range(CB):
             seq_bf = held.tile([P, N], BF16, name=f"seq_bf{kb}")

@@ -39,7 +39,8 @@ def tile_att_diffuse_model_kernel(tc, item_emb, pos_emb, wk, bk, wv, bv, offs, o
         biases = {}
         for name, b in (("k", bk), ("v", bv)):
             biases[name] = held.tile([P, CB], F32, name=f"b{name}")
-            queues[name].dma_start(biases[name][:], b.rearrange("(p mb) o -> p (mb o)", p=P))
+            with nc.allow_non_contiguous_dma(reason="256 biases, one to a partition and block"):
+                queues[name].dma_start(biases[name][:], b.rearrange("(mb p) o -> p (mb o)", p=P))
 
         zeros = held.tile([P, WARM_COLUMNS], BF16, name="zeros")
         nc.vector.memset(zeros[:], 0.0)
@@ -65,7 +66,7 @@ def tile_att_diffuse_model_kernel(tc, item_emb, pos_emb, wk, bk, wv, bv, offs, o
             for name, mb in blocks:
                 nc.tensor.matmul(
                     products[name, mb][:],
-                    weights[name][:, kb, mb::CB],
+                    weights[name][:, kb, mb * P : (mb + 1) * P],
                     seq_bf[:],
                     start=(kb == 0),
                     stop=(kb == CB - 1),
@@ -80,4 +81,4 @@ def tile_att_diffuse_model_kernel(tc, item_emb, pos_emb, wk, bk, wv, bv, offs, o
                 else:
                     nc.scalar.activation(biased[:, mb, :], products[name, mb][:], identity, bias=bias)
             rows = out[(1 + part) * C : (2 + part) * C, :]
-            queues[name].dma_start(rows.rearrange("(p mb) n -> p mb n", p=P), biased[:])
+            queues[name].dma_start(rows.rearrange("(mb p) n -> p mb n", p=P), biased[:])

import concourse.mybir as mybir

P = 128
C, S, N = 256, 256, 128
CB = C // P
F32, BF16, U16 = mybir.dt.float32, mybir.dt.bfloat16, mybir.dt.uint16

WARM_COLUMNS = 512
WARM_MATMULS = 5

FLOPS = 2 * (2 * C) * C * N


def tile_att_diffuse_model_kernel(tc, item_emb, pos_emb, wk, bk, wv, bv, offs, out):
    nc = tc.nc
    add = mybir.AluOpType.add
    identity = mybir.ActivationFunctionType.Identity

    with (
        tc.tile_pool(name="held", bufs=1) as held,
        tc.psum_pool(name="psum", bufs=1) as psum,
    ):
        item_rows = item_emb.rearrange("(p cb) s -> p cb s", p=P)
        items = [held.tile([P, S], F32, name=f"items{cb}") for cb in range(CB)]
        offsets = held.tile([P, N // 16], U16, name="offsets")
        pos = held.tile([P, CB, N], F32, name="pos")
        nc.sync.dma_start(items[0][:], item_rows[:, 0, :])
        nc.sync.dma_start(offsets[:], offs)
        nc.scalar.dma_start(pos[:], pos_emb.rearrange("(p cb) n -> p cb n", p=P))
        nc.scalar.dma_start(items[1][:], item_rows[:, 1, :])

        queues = {"k": nc.sync, "v": nc.scalar}

        weights = {}
        for name, w in (("k", wk), ("v", wv)):
            weights[name] = held.tile([P, CB, C], BF16, name=f"w{name}")
            queues[name].dma_start(weights[name][:], w.rearrange("(p kb) m -> p kb m", p=P))

        biases = {}
        for name, b in (("k", bk), ("v", bv)):
            biases[name] = held.tile([P, CB], F32, name=f"b{name}")
            with nc.allow_non_contiguous_dma(reason="256 biases, one to a partition and block"):
                queues[name].dma_start(biases[name][:], b.rearrange("(mb p) o -> p (mb o)", p=P))

        zeros = held.tile([P, WARM_COLUMNS], BF16, name="zeros")
        nc.vector.memset(zeros[:], 0.0)
        unused = psum.tile([P, WARM_COLUMNS], F32, name="unused")
        for repeat in range(WARM_MATMULS):
            nc.tensor.matmul(unused[:], zeros[:, 0:P], zeros[:], start=True, stop=True)

        unused_column = held.tile([P, 1], F32, name="unused_column")
        nc.scalar.activation(unused_column[:], zeros[:, 0:1], identity)

        blocks = [(name, mb) for name in ("k", "v") for mb in range(CB)]
        products = {block: psum.tile([P, N], F32, name=f"product_{block[0]}{block[1]}") for block in blocks}

        seq_rows = out[0:C, :].rearrange("(p cb) n -> p cb n", p=P)
        seq = [held.tile([P, N], F32, name=f"seq{cb}") for cb in range(CB)]
        for cb in range(CB):
            nc.vector.tensor_tensor(seq[cb][:], items[cb][:].indirect(offsets[:]), pos[:, cb, :], add)
            (nc.sync, nc.scalar)[cb].dma_start(seq_rows[:, cb, :], seq[cb][:])

        for kb in range(CB):
            seq_bf = held.tile([P, N], BF16, name=f"seq_bf{kb}")
            nc.vector.tensor_copy(seq_bf[:], seq[kb][:])
            for name, mb in blocks:
                nc.tensor.matmul(
                    products[name, mb][:],
                    weights[name][:, kb, mb * P : (mb + 1) * P],
                    seq_bf[:],
                    start=(kb == 0),
                    stop=(kb == CB - 1),
                )

        for part, name in enumerate(("k", "v")):
            biased = held.tile([P, CB, N], F32, name=f"biased_{name}")
            for mb in range(CB):
                bias = biases[name][:, mb : mb + 1]
                if name == "k":
                    nc.vector.tensor_scalar(biased[:, mb, :], products[name, mb][:], bias, None, add)
                else:
                    nc.scalar.activation(biased[:, mb, :], products[name, mb][:], identity, bias=bias)
            rows = out[(1 + part) * C : (2 + part) * C, :]
            queues[name].dma_start(rows.rearrange("(mb p) n -> p mb n", p=P), biased[:])
